import numpy as np
import ml_dtypes


def mxq(x, axis, fmt="e4m3"):
    dtype, down = {"e4m3": (ml_dtypes.float8_e4m3fn, 7), "e5m2": (ml_dtypes.float8_e5m2, 14)}[fmt]
    v = np.moveaxis(np.asarray(x, np.float32).astype(ml_dtypes.bfloat16).astype(np.float64), axis, -1)
    blocks = v.reshape(v.shape[:-1] + (-1, 32))
    amax = np.abs(blocks).max(-1, keepdims=True)
    byte = np.maximum(np.where(amax > 0, np.frexp(amax)[1] - 1 + 127, 0) - down, 1)
    scale = np.exp2(byte - 127.0)
    codes = (blocks / scale).astype(np.float32).astype(dtype).astype(np.float64)
    return np.moveaxis((codes * scale).reshape(v.shape), -1, axis)


WIDE = False


def mx_kscale(k):
    if not WIDE:
        return np.ones(k)
    levels = np.array([10, -10, 5, -5, 0])
    a = np.random.permutation(np.resize(levels, k // 512 * 4)).reshape(k // 512, 4)
    idx = np.arange(k)
    return np.exp2(a[idx // 512, idx % 128 // 32])


BF16 = ml_dtypes.bfloat16


def bf(x):
    return np.asarray(x, np.float32).astype(BF16)


def f64(x):
    return np.asarray(x).astype(np.float64)


B, N, HD, ED, F = 1, 64, 128, 256, 1024
TD = HD + HD
MD = TD + ED
EPS = 1e-5


def layer_norm(x, g, b):
    mu = x.mean(-1, keepdims=True)
    var = x.var(-1, keepdims=True)
    return (x - mu) * (1.0 / np.sqrt(var + EPS)) * g + b


def setup_inputs():
    s = mx_kscale(MD)
    sx, se = s[:HD], s[TD:]
    sr = np.concatenate([sx, sx, se])
    return {"p": bf(np.random.standard_normal((B, N, N, ED)) + 0.5 * np.random.standard_normal((B, N, N))[..., None]),
            "x_down": bf(np.random.standard_normal((B, N, HD)) * sx),
            "ln_edge_g": bf((1.0 + 0.1 * np.random.standard_normal(ED)) * se),
            "ln_edge_b": bf(0.1 * np.random.standard_normal(ED) * se),
            "W1": bf(np.random.standard_normal((MD, F)) / np.sqrt(MD) / sr[:, None]),
            "b1": bf(0.1 * np.random.standard_normal(F))}


def reference(p, x_down, ln_edge_g, ln_edge_b, W1, b1):
    p_ln = layer_norm(f64(p), f64(ln_edge_g), f64(ln_edge_b))
    xd = f64(x_down)
    edge_bias = np.concatenate([np.broadcast_to(xd[:, :, None, :], (B, N, N, HD)),
                                np.broadcast_to(xd[:, None, :, :], (B, N, N, HD))], axis=-1)
    z_in = np.concatenate([edge_bias, p_ln], axis=-1)
    return np.maximum((mxq(z_in, 3, "e4m3") @ mxq(f64(W1), 0, "e4m3")) + f64(b1), 0.0)

@@ -1,0 +1,169 @@
+import concourse.mybir as mybir
+from concourse.masks import make_identity
+
+F32 = mybir.dt.float32
+BF16 = mybir.dt.bfloat16
+U32 = mybir.dt.uint32
+U8 = mybir.dt.uint8
+FP8X4 = mybir.dt.float8_e4m3fn_x4
+ALU = mybir.AluOpType
+ACT = mybir.ActivationFunctionType
+
+P = 128
+PACK = 4
+NODES = 64
+HD = 128
+ED = 256
+F = 1024
+EDGES = NODES * NODES
+TILES = EDGES // P
+N_BANK = 512
+EPS = 1e-5
+PAIR = 2
+QUAD = 4
+FILL = 8
+
+FLOPS = 2 * EDGES * (2 * HD + ED) * F
+
+
+def tile_edgeupdaterwrapper_v01_pa_t_kernel(tc, p, x_down, ln_edge_g, ln_edge_b, W1, b1, out):
+    nc = tc.nc
+    p_view = p.rearrange("b i j f -> (b i j) f").rearrange("(m t) f -> m t f", t=TILES)
+    out_view = out.rearrange("b i j f -> (b i j) f").rearrange("(m t) f -> m t f", t=TILES)
+
+    with tc.tile_pool(name="keep", bufs=1) as keep:
+        small = keep.tile([P, HD], BF16)
+        nc.vector.memset(small[NODES:P, :], 0.0)
+        nc.sync.dma_start(out=small[0:NODES, :], in_=x_down.rearrange("b n f -> (b n) f"))
+        nc.sync.dma_start(out=small[NODES : NODES + 2, :], in_=ln_edge_g.rearrange("(h q) -> h q", q=P))
+        nc.sync.dma_start(out=small[NODES + 2 : NODES + 4, :], in_=ln_edge_b.rearrange("(h q) -> h q", q=P))
+        w_view = W1.rearrange("(t q) n -> q t n", q=P)
+        w_raw = keep.tile([P, PACK, F], BF16)
+        p_sb = keep.tile([P, TILES, ED], BF16)
+        b1_bc = keep.tile([P, F], BF16)
+        nc.sync.dma_start(out=w_raw[:, :, 0:N_BANK], in_=w_view[:, :, 0:N_BANK])
+        nc.sync.dma_start(out=p_sb[:, 0:FILL, :], in_=p_view[:, 0:FILL, :])
+        nc.sync.dma_start(out=w_raw[:, :, N_BANK:F], in_=w_view[:, :, N_BANK:F])
+        nc.sync.dma_start(out=b1_bc[:], in_=b1.partition_broadcast(P))
+        for c in range(1, TILES // FILL):
+            nc.sync.dma_start(out=p_sb[:, c * FILL : (c + 1) * FILL, :], in_=p_view[:, c * FILL : (c + 1) * FILL, :])
+
+        ident_bf = keep.tile([P, P], BF16)
+        make_identity(nc, ident_bf[:])
+        ident_f32 = keep.tile([P, P], F32)
+        make_identity(nc, ident_f32[:])
+        eps = keep.tile([P, 1], F32)
+        nc.vector.memset(eps[:], EPS)
+
+        x_t = keep.tile([P, NODES], BF16)
+        gain_bias = keep.tile([P, 4], F32)
+        with tc.psum_pool(name="psum_setup", bufs=1) as psum_setup:
+            small_t = psum_setup.tile([P, P], BF16)
+            nc.tensor.transpose(out=small_t[:], in_=small[:], identity=ident_bf[:])
+            nc.vector.tensor_copy(out=x_t[:], in_=small_t[:, 0:NODES])
+            nc.vector.tensor_copy(out=gain_bias[:], in_=small_t[:, NODES : NODES + 4])
+
+        w_grouped = keep.tile([P, F, PACK], BF16, align_bytes=64)
+        w_codes = keep.tile([P, F], U32, align_bytes=64)
+        w_scales = keep.tile([P, F], U8, align_bytes=64)
+        for nh in range(F // N_BANK):
+            cols = slice(nh * N_BANK, (nh + 1) * N_BANK)
+            nc.vector.tensor_copy(out=w_grouped[:, cols, :], in_=w_raw[:, :, cols].rearrange("q t n -> q n t"))
+        for nh in range(F // N_BANK):
+            cols = slice(nh * N_BANK, (nh + 1) * N_BANK)
+            nc.vector.quantize_mx(
+                out=w_codes[:, cols].bitcast(FP8X4),
+                scales=w_scales[:, cols],
+                in_=w_grouped[:, cols, :].rearrange("q n t -> q (n t)"),
+            )
+
+        planes = keep.tile([P, TILES, PACK, P], BF16)
+        x_j_view = x_t[:].rearrange("q (a t) -> q t a", t=TILES)
+        for c in range(TILES // FILL):
+            ts = slice(c * FILL, (c + 1) * FILL)
+            nc.gpsimd.tensor_scalar(
+                out=planes[:, ts, 0, :].rearrange("q t (i a) -> q t i a", a=2),
+                in0=x_t[:].unsqueeze(1).unsqueeze(3).to_broadcast([P, FILL, NODES, 2]),
+                scalar1=1.0, scalar2=0.0, op0=ALU.mult, op1=ALU.add,
+            )
+            nc.gpsimd.tensor_scalar(
+                out=planes[:, ts, 1, :].rearrange("q t (i a) -> q t i a", a=2),
+                in0=x_j_view[:, ts, :].unsqueeze(2).to_broadcast([P, FILL, NODES, 2]),
+                scalar1=1.0, scalar2=0.0, op0=ALU.mult, op1=ALU.add,
+            )
+
+        stats = keep.tile([P, TILES, 6], F32)
+        mean_var = keep.tile([P, TILES, 2], F32)
+        std = keep.tile([P, TILES], F32)
+        rstd = keep.tile([P, TILES], F32)
+        shift = keep.tile([P, TILES], F32)
+
+        with tc.tile_pool(name="work", bufs=3) as work, tc.tile_pool(name="outs", bufs=6) as outs, \
+                tc.psum_pool(name="psum_t", bufs=2) as psum_t, tc.psum_pool(name="psum_mm", bufs=6) as psum_mm:
+
+            def statistics(quad):
+                ts = slice(quad * QUAD, (quad + 1) * QUAD)
+                for t in range(quad * QUAD, (quad + 1) * QUAD):
+                    nc.vector.bn_stats(out=stats[:, t, :], in_=p_sb[:, t, :])
+                    nc.vector.bn_aggr(out=mean_var[:, t, :], in_=stats[:, t, :])
+                nc.scalar.activation(out=std[:, ts], in_=mean_var[:, ts, 1], func=ACT.Sqrt, bias=eps[:, 0:1], scale=1.0)
+                nc.vector.reciprocal(out=rstd[:, ts], in_=std[:, ts])
+                nc.vector.scalar_tensor_tensor(
+                    out=shift[:, ts], in0=mean_var[:, ts, 0], scalar=-1.0, in1=rstd[:, ts], op0=ALU.mult, op1=ALU.mult
+                )
+
+            def quantise_pair(pair):
+                t0 = pair * PAIR
+                normed = work.tile([P, PAIR, ED], F32)
+                for a in range(PAIR):
+                    t = t0 + a
+                    nc.scalar.activation(
+                        out=normed[:, a, :], in_=p_sb[:, t, :], func=ACT.Identity,
+                        bias=shift[:, t : t + 1], scale=rstd[:, t : t + 1],
+                    )
+                normed_t = psum_t.tile([P, 2, PAIR, P], F32)
+                for h in range(2):
+                    for a in range(PAIR):
+                        nc.tensor.transpose(
+                            out=normed_t[:, h, a, :], in_=normed[:, a, h * P : (h + 1) * P], identity=ident_f32[:]
+                        )
+                for h in range(2):
+                    nc.scalar.activation(
+                        out=planes[:, t0 : t0 + PAIR, 2 + h, :], in_=normed_t[:, h, :, :], func=ACT.Identity,
+                        bias=gain_bias[:, 2 + h : 3 + h], scale=gain_bias[:, h : h + 1],
+                    )
+                grouped = work.tile([P, PAIR, P, PACK], BF16, align_bytes=64)
+                nc.scalar.copy(out=grouped[:], in_=planes[:, t0 : t0 + PAIR, :, :].rearrange("q a t m -> q a m t"))
+                z_codes = work.tile([P, PAIR * P], U32, align_bytes=64)
+                z_scales = work.tile([P, PAIR * P], U8, align_bytes=64)
+                nc.vector.quantize_mx(
+                    out=z_codes[:].bitcast(FP8X4), scales=z_scales[:], in_=grouped[:].rearrange("q a m t -> q (a m t)")
+                )
+                return z_codes, z_scales
+
+            def multiply_pair(pair, z_codes, z_scales):
+                t0 = pair * PAIR
+                result = outs.tile([P, PAIR, F], F32)
+                for a in range(PAIR):
+                    edges = slice(a * P, (a + 1) * P)
+                    for nh in range(F // N_BANK):
+                        cols = slice(nh * N_BANK, (nh + 1) * N_BANK)
+                        acc = psum_mm.tile([P, N_BANK], F32)
+                        nc.tensor.matmul_mx(
+                            out=acc[:],
+                            lhsT=z_codes[:, edges].bitcast(FP8X4), lhsT_scale=z_scales[:, edges],
+                            rhs=w_codes[:, cols].bitcast(FP8X4), rhs_scale=w_scales[:, cols],
+                            start=True, stop=True,
+                        )
+                        nc.vector.tensor_tensor(out=result[:, a, cols], in0=acc[:], in1=b1_bc[:, cols], op=ALU.add)
+                    nc.gpsimd.tensor_scalar(
+                        out=result[:, a, :], in0=result[:, a, :],
+                        scalar1=float("inf"), scalar2=0.0, op0=ALU.min, op1=ALU.max,
+                    )
+                nc.sync.dma_start(out=out_view[:, t0 : t0 + PAIR, :], in_=result[:])
+
+            for pair in range(TILES // PAIR):
+                if pair % (QUAD // PAIR) == 0:
+                    statistics(pair // (QUAD // PAIR))
+                z_codes, z_scales = quantise_pair(pair)
+                multiply_pair(pair, z_codes, z_scales)

@@ -20,8 +20,10 @@ TILES = EDGES // P
 N_BANK = 512
 EPS = 1e-5
 PAIR = 2
-QUAD = 4
+PAIRS = TILES // PAIR
+LOAD = 4
 FILL = 8
+LAG = 2
 
 FLOPS = 2 * EDGES * (2 * HD + ED) * F
 
@@ -31,7 +33,7 @@ def tile_edgeupdaterwrapper_v01_pa_t_kernel(tc, p, x_down, ln_edge_g, ln_edge_b,
     p_view = p.rearrange("b i j f -> (b i j) f").rearrange("(m t) f -> m t f", t=TILES)
     out_view = out.rearrange("b i j f -> (b i j) f").rearrange("(m t) f -> m t f", t=TILES)
 
-    with tc.tile_pool(name="keep", bufs=1) as keep:
+    with tc.manual_schedule(), tc.tile_pool(name="keep", bufs=1) as keep:
         small = keep.tile([P, HD], BF16)
         nc.vector.memset(small[NODES:P, :], 0.0)
         nc.sync.dma_start(out=small[0:NODES, :], in_=x_down.rearrange("b n f -> (b n) f"))
@@ -41,12 +43,17 @@ def tile_edgeupdaterwrapper_v01_pa_t_kernel(tc, p, x_down, ln_edge_g, ln_edge_b,
         w_raw = keep.tile([P, PACK, F], BF16)
         p_sb = keep.tile([P, TILES, ED], BF16)
         b1_bc = keep.tile([P, F], BF16)
+
+        def load_p(c):
+            nc.sync.dma_start(out=p_sb[:, c * LOAD : (c + 1) * LOAD, :], in_=p_view[:, c * LOAD : (c + 1) * LOAD, :])
+
+        load_p(0)
+        load_p(1)
         nc.sync.dma_start(out=w_raw[:, :, 0:N_BANK], in_=w_view[:, :, 0:N_BANK])
-        nc.sync.dma_start(out=p_sb[:, 0:FILL, :], in_=p_view[:, 0:FILL, :])
         nc.sync.dma_start(out=w_raw[:, :, N_BANK:F], in_=w_view[:, :, N_BANK:F])
         nc.sync.dma_start(out=b1_bc[:], in_=b1.partition_broadcast(P))
-        for c in range(1, TILES // FILL):
-            nc.sync.dma_start(out=p_sb[:, c * FILL : (c + 1) * FILL, :], in_=p_view[:, c * FILL : (c + 1) * FILL, :])
+        for c in range(2, TILES // LOAD):
+            load_p(c)
 
         ident_bf = keep.tile([P, P], BF16)
         make_identity(nc, ident_bf[:])
@@ -63,20 +70,6 @@ def tile_edgeupdaterwrapper_v01_pa_t_kernel(tc, p, x_down, ln_edge_g, ln_edge_b,
             nc.vector.tensor_copy(out=x_t[:], in_=small_t[:, 0:NODES])
             nc.vector.tensor_copy(out=gain_bias[:], in_=small_t[:, NODES : NODES + 4])
 
-        w_grouped = keep.tile([P, F, PACK], BF16, align_bytes=64)
-        w_codes = keep.tile([P, F], U32, align_bytes=64)
-        w_scales = keep.tile([P, F], U8, align_bytes=64)
-        for nh in range(F // N_BANK):
-            cols = slice(nh * N_BANK, (nh + 1) * N_BANK)
-            nc.vector.tensor_copy(out=w_grouped[:, cols, :], in_=w_raw[:, :, cols].rearrange("q t n -> q n t"))
-        for nh in range(F // N_BANK):
-            cols = slice(nh * N_BANK, (nh + 1) * N_BANK)
-            nc.vector.quantize_mx(
-                out=w_codes[:, cols].bitcast(FP8X4),
-                scales=w_scales[:, cols],
-                in_=w_grouped[:, cols, :].rearrange("q n t -> q (n t)"),
-            )
-
         planes = keep.tile([P, TILES, PACK, P], BF16)
         x_j_view = x_t[:].rearrange("q (a t) -> q t a", t=TILES)
         for c in range(TILES // FILL):
@@ -92,78 +85,161 @@ def tile_edgeupdaterwrapper_v01_pa_t_kernel(tc, p, x_down, ln_edge_g, ln_edge_b,
                 scalar1=1.0, scalar2=0.0, op0=ALU.mult, op1=ALU.add,
             )
 
+        w_grouped = keep.tile([P, F, PACK], BF16, align_bytes=64)
+        w_codes = keep.tile([P, F], U32, align_bytes=64)
+        w_scales = keep.tile([P, F], U8, align_bytes=64)
+
+        def prepare_weights():
+            for nh in range(F // N_BANK):
+                cols = slice(nh * N_BANK, (nh + 1) * N_BANK)
+                nc.vector.tensor_copy(out=w_grouped[:, cols, :], in_=w_raw[:, :, cols].rearrange("q t n -> q n t"))
+            for nh in range(F // N_BANK):
+                cols = slice(nh * N_BANK, (nh + 1) * N_BANK)
+                nc.vector.quantize_mx(
+                    out=w_codes[:, cols].bitcast(FP8X4),
+                    scales=w_scales[:, cols],
+                    in_=w_grouped[:, cols, :].rearrange("q n t -> q (n t)"),
+                )
+
         stats = keep.tile([P, TILES, 6], F32)
         mean_var = keep.tile([P, TILES, 2], F32)
         std = keep.tile([P, TILES], F32)
         rstd = keep.tile([P, TILES], F32)
         shift = keep.tile([P, TILES], F32)
 
-        with tc.tile_pool(name="work", bufs=3) as work, tc.tile_pool(name="outs", bufs=6) as outs, \
+        with tc.tile_pool(name="work", bufs=3) as work, tc.tile_pool(name="outs", bufs=8) as outs, \
                 tc.psum_pool(name="psum_t", bufs=2) as psum_t, tc.psum_pool(name="psum_mm", bufs=6) as psum_mm:
+            normed_of = {}
+            normed_t_of = {}
+            grouped_of = {}
+            z_of = {}
+            acc_of = {}
+            result_of = {}
 
-            def statistics(quad):
-                ts = slice(quad * QUAD, (quad + 1) * QUAD)
-                for t in range(quad * QUAD, (quad + 1) * QUAD):
+            def tiles_of(k):
+                return slice(k * PAIR, (k + 1) * PAIR)
+
+            def mean_and_variance(k):
+                for t in range(k * PAIR, (k + 1) * PAIR):
                     nc.vector.bn_stats(out=stats[:, t, :], in_=p_sb[:, t, :])
                     nc.vector.bn_aggr(out=mean_var[:, t, :], in_=stats[:, t, :])
+
+            def standard_deviation(k):
+                ts = tiles_of(k)
                 nc.scalar.activation(out=std[:, ts], in_=mean_var[:, ts, 1], func=ACT.Sqrt, bias=eps[:, 0:1], scale=1.0)
+
+            def scale_and_shift(k):
+                ts = tiles_of(k)
                 nc.vector.reciprocal(out=rstd[:, ts], in_=std[:, ts])
                 nc.vector.scalar_tensor_tensor(
                     out=shift[:, ts], in0=mean_var[:, ts, 0], scalar=-1.0, in1=rstd[:, ts], op0=ALU.mult, op1=ALU.mult
                 )
 
-            def quantise_pair(pair):
-                t0 = pair * PAIR
+            def normalise(k):
                 normed = work.tile([P, PAIR, ED], F32)
                 for a in range(PAIR):
-                    t = t0 + a
+                    t = k * PAIR + a
                     nc.scalar.activation(
                         out=normed[:, a, :], in_=p_sb[:, t, :], func=ACT.Identity,
                         bias=shift[:, t : t + 1], scale=rstd[:, t : t + 1],
                     )
+                normed_of[k] = normed
+
+            def transpose(k):
+                normed = normed_of.pop(k)
                 normed_t = psum_t.tile([P, 2, PAIR, P], F32)
                 for h in range(2):
                     for a in range(PAIR):
                         nc.tensor.transpose(
                             out=normed_t[:, h, a, :], in_=normed[:, a, h * P : (h + 1) * P], identity=ident_f32[:]
                         )
+                normed_t_of[k] = normed_t
+
+            def group(k):
+                normed_t = normed_t_of.pop(k)
                 for h in range(2):
                     nc.scalar.activation(
-                        out=planes[:, t0 : t0 + PAIR, 2 + h, :], in_=normed_t[:, h, :, :], func=ACT.Identity,
+                        out=planes[:, tiles_of(k), 2 + h, :], in_=normed_t[:, h, :, :], func=ACT.Identity,
                         bias=gain_bias[:, 2 + h : 3 + h], scale=gain_bias[:, h : h + 1],
                     )
                 grouped = work.tile([P, PAIR, P, PACK], BF16, align_bytes=64)
-                nc.scalar.copy(out=grouped[:], in_=planes[:, t0 : t0 + PAIR, :, :].rearrange("q a t m -> q a m t"))
+                nc.scalar.copy(out=grouped[:], in_=planes[:, tiles_of(k), :, :].rearrange("q a t m -> q a m t"))
+                grouped_of[k] = grouped
+
+            def quantise(k):
+                grouped = grouped_of.pop(k)
                 z_codes = work.tile([P, PAIR * P], U32, align_bytes=64)
                 z_scales = work.tile([P, PAIR * P], U8, align_bytes=64)
                 nc.vector.quantize_mx(
                     out=z_codes[:].bitcast(FP8X4), scales=z_scales[:], in_=grouped[:].rearrange("q a m t -> q (a m t)")
                 )
-                return z_codes, z_scales
+                z_of[k] = (z_codes, z_scales)
 
-            def multiply_pair(pair, z_codes, z_scales):
-                t0 = pair * PAIR
-                result = outs.tile([P, PAIR, F], F32)
-                for a in range(PAIR):
-                    edges = slice(a * P, (a + 1) * P)
-                    for nh in range(F // N_BANK):
-                        cols = slice(nh * N_BANK, (nh + 1) * N_BANK)
-                        acc = psum_mm.tile([P, N_BANK], F32)
-                        nc.tensor.matmul_mx(
-                            out=acc[:],
-                            lhsT=z_codes[:, edges].bitcast(FP8X4), lhsT_scale=z_scales[:, edges],
-                            rhs=w_codes[:, cols].bitcast(FP8X4), rhs_scale=w_scales[:, cols],
-                            start=True, stop=True,
-                        )
-                        nc.vector.tensor_tensor(out=result[:, a, cols], in0=acc[:], in1=b1_bc[:, cols], op=ALU.add)
-                    nc.gpsimd.tensor_scalar(
-                        out=result[:, a, :], in0=result[:, a, :],
-                        scalar1=float("inf"), scalar2=0.0, op0=ALU.min, op1=ALU.max,
+            def multiply(t):
+                z_codes, z_scales = z_of[t // PAIR]
+                edges = slice((t % PAIR) * P, (t % PAIR + 1) * P)
+                for nh in range(F // N_BANK):
+                    cols = slice(nh * N_BANK, (nh + 1) * N_BANK)
+                    acc = psum_mm.tile([P, N_BANK], F32)
+                    nc.tensor.matmul_mx(
+                        out=acc[:],
+                        lhsT=z_codes[:, edges].bitcast(FP8X4), lhsT_scale=z_scales[:, edges],
+                        rhs=w_codes[:, cols].bitcast(FP8X4), rhs_scale=w_scales[:, cols],
+                        start=True, stop=True,
                     )
-                nc.sync.dma_start(out=out_view[:, t0 : t0 + PAIR, :], in_=result[:])
+                    acc_of[(t, nh)] = acc
 
-            for pair in range(TILES // PAIR):
-                if pair % (QUAD // PAIR) == 0:
-                    statistics(pair // (QUAD // PAIR))
-                z_codes, z_scales = quantise_pair(pair)
-                multiply_pair(pair, z_codes, z_scales)
+            def add_bias(t):
+                result = outs.tile([P, F], F32)
+                for nh in range(F // N_BANK):
+                    cols = slice(nh * N_BANK, (nh + 1) * N_BANK)
+                    nc.vector.tensor_tensor(out=result[:, cols], in0=acc_of.pop((t, nh))[:], in1=b1_bc[:, cols], op=ALU.add)
+                result_of[t] = result
+
+            def relu_and_store(t):
+                result = result_of.pop(t)
+                nc.gpsimd.tensor_scalar(
+                    out=result[:], in0=result[:], scalar1=float("inf"), scalar2=0.0, op0=ALU.min, op1=ALU.max
+                )
+                nc.sync.dma_start(out=out_view[:, t, :], in_=result[:])
+
+            def is_pair(k):
+                return 0 <= k < PAIRS
+
+            def is_tile(t):
+                return 0 <= t < TILES
+
+            mean_and_variance(0)
+            standard_deviation(0)
+            mean_and_variance(1)
+            standard_deviation(1)
+            scale_and_shift(0)
+            for n in range(PAIRS + 4):
+                first = (n - LAG) * PAIR
+                if n == LAG:
+                    prepare_weights()
+                if is_pair(n - LAG):
+                    quantise(n - LAG)
+                if is_pair(n):
+                    normalise(n)
+                if is_pair(n - LAG):
+                    multiply(first)
+                    multiply(first + 1)
+                if is_pair(n):
+                    transpose(n)
+                if is_tile(first - 1):
+                    add_bias(first - 1)
+                if is_tile(first - 2):
+                    relu_and_store(first - 2)
+                if is_pair(n + 1):
+                    scale_and_shift(n + 1)
+                if is_pair(n + 2):
+                    mean_and_variance(n + 2)
+                if is_pair(n - 1):
+                    group(n - 1)
+                if is_tile(first):
+                    add_bias(first)
+                if is_tile(first - 1):
+                    relu_and_store(first - 1)
+                if is_pair(n + 2):
+                    standard_deviation(n + 2)

@@ -24,6 +24,7 @@ PAIRS = TILES // PAIR
 LOAD = 4
 FILL = 8
 LAG = 2
+SCALAR_COLS = 384
 
 FLOPS = 2 * EDGES * (2 * HD + ED) * F
 
@@ -198,8 +199,10 @@ def tile_edgeupdaterwrapper_v01_pa_t_kernel(tc, p, x_down, ln_edge_g, ln_edge_b,
 
             def relu_and_store(t):
                 result = result_of.pop(t)
+                nc.scalar.activation(out=result[:, 0:SCALAR_COLS], in_=result[:, 0:SCALAR_COLS], func=ACT.Relu)
                 nc.gpsimd.tensor_scalar(
-                    out=result[:], in0=result[:], scalar1=float("inf"), scalar2=0.0, op0=ALU.min, op1=ALU.max
+                    out=result[:, SCALAR_COLS:F], in0=result[:, SCALAR_COLS:F],
+                    scalar1=float("inf"), scalar2=0.0, op0=ALU.min, op1=ALU.max,
                 )
                 nc.sync.dma_start(out=out_view[:, t, :], in_=result[:])
 

@@ -104,7 +104,6 @@ def tile_edgeupdaterwrapper_v01_pa_t_kernel(tc, p, x_down, ln_edge_g, ln_edge_b,
 
         stats = keep.tile([P, TILES, 6], F32)
         mean_var = keep.tile([P, TILES, 2], F32)
-        std = keep.tile([P, TILES], F32)
         rstd = keep.tile([P, TILES], F32)
         shift = keep.tile([P, TILES], F32)
 
@@ -120,18 +119,22 @@ def tile_edgeupdaterwrapper_v01_pa_t_kernel(tc, p, x_down, ln_edge_g, ln_edge_b,
             def tiles_of(k):
                 return slice(k * PAIR, (k + 1) * PAIR)
 
-            def mean_and_variance(k):
+            def sums(k):
                 for t in range(k * PAIR, (k + 1) * PAIR):
                     nc.vector.bn_stats(out=stats[:, t, :], in_=p_sb[:, t, :])
+
+            def mean_and_variance(k):
+                for t in range(k * PAIR, (k + 1) * PAIR):
                     nc.vector.bn_aggr(out=mean_var[:, t, :], in_=stats[:, t, :])
 
-            def standard_deviation(k):
+            def scale(k):
                 ts = tiles_of(k)
-                nc.scalar.activation(out=std[:, ts], in_=mean_var[:, ts, 1], func=ACT.Sqrt, bias=eps[:, 0:1], scale=1.0)
+                nc.scalar.activation(
+                    out=rstd[:, ts], in_=mean_var[:, ts, 1], func=ACT.Abs_reciprocal_sqrt, bias=eps[:, 0:1], scale=1.0
+                )
 
-            def scale_and_shift(k):
+            def shift_by_mean(k):
                 ts = tiles_of(k)
-                nc.vector.reciprocal(out=rstd[:, ts], in_=std[:, ts])
                 nc.vector.scalar_tensor_tensor(
                     out=shift[:, ts], in0=mean_var[:, ts, 0], scalar=-1.0, in1=rstd[:, ts], op0=ALU.mult, op1=ALU.mult
                 )
@@ -190,12 +193,13 @@ def tile_edgeupdaterwrapper_v01_pa_t_kernel(tc, p, x_down, ln_edge_g, ln_edge_b,
                     )
                     acc_of[(t, nh)] = acc
 
-            def add_bias(t):
-                result = outs.tile([P, F], F32)
-                for nh in range(F // N_BANK):
-                    cols = slice(nh * N_BANK, (nh + 1) * N_BANK)
-                    nc.vector.tensor_tensor(out=result[:, cols], in0=acc_of.pop((t, nh))[:], in1=b1_bc[:, cols], op=ALU.add)
-                result_of[t] = result
+            def add_bias(t, nh):
+                if nh == 0:
+                    result_of[t] = outs.tile([P, F], F32, name="result")
+                cols = slice(nh * N_BANK, (nh + 1) * N_BANK)
+                nc.vector.tensor_tensor(
+                    out=result_of[t][:, cols], in0=acc_of.pop((t, nh))[:], in1=b1_bc[:, cols], op=ALU.add
+                )
 
             def relu_and_store(t):
                 result = result_of.pop(t)
@@ -212,17 +216,20 @@ def tile_edgeupdaterwrapper_v01_pa_t_kernel(tc, p, x_down, ln_edge_g, ln_edge_b,
             def is_tile(t):
                 return 0 <= t < TILES
 
-            mean_and_variance(0)
-            standard_deviation(0)
-            mean_and_variance(1)
-            standard_deviation(1)
-            scale_and_shift(0)
-            for n in range(PAIRS + 4):
+            for k in range(2):
+                sums(k)
+            for k in range(2):
+                mean_and_variance(k)
+            scale(0)
+            shift_by_mean(0)
+            for n in range(PAIRS + 3):
                 first = (n - LAG) * PAIR
                 if n == LAG:
                     prepare_weights()
                 if is_pair(n - LAG):
                     quantise(n - LAG)
+                if is_pair(n + 1):
+                    scale(n + 1)
                 if is_pair(n):
                     normalise(n)
                 if is_pair(n - LAG):
@@ -231,18 +238,21 @@ def tile_edgeupdaterwrapper_v01_pa_t_kernel(tc, p, x_down, ln_edge_g, ln_edge_b,
                 if is_pair(n):
                     transpose(n)
                 if is_tile(first - 1):
-                    add_bias(first - 1)
+                    add_bias(first - 1, 0)
+                    add_bias(first - 1, 1)
                 if is_tile(first - 2):
                     relu_and_store(first - 2)
-                if is_pair(n + 1):
-                    scale_and_shift(n + 1)
                 if is_pair(n + 2):
-                    mean_and_variance(n + 2)
+                    sums(n + 2)
+                if is_pair(n + 1):
+                    shift_by_mean(n + 1)
                 if is_pair(n - 1):
                     group(n - 1)
                 if is_tile(first):
-                    add_bias(first)
+                    add_bias(first, 0)
+                if is_pair(n + 2):
+                    mean_and_variance(n + 2)
+                if is_tile(first):
+                    add_bias(first, 1)
                 if is_tile(first - 1):
                     relu_and_store(first - 1)
-                if is_pair(n + 2):
-                    standard_deviation(n + 2)

@@ -24,7 +24,7 @@ PAIRS = TILES // PAIR
 LOAD = 4
 FILL = 8
 LAG = 2
-SCALAR_COLS = 384
+SCALAR_COLS = 768
 
 FLOPS = 2 * EDGES * (2 * HD + ED) * F
 
@@ -159,15 +159,20 @@ def tile_edgeupdaterwrapper_v01_pa_t_kernel(tc, p, x_down, ln_edge_g, ln_edge_b,
                         )
                 normed_t_of[k] = normed_t
 
-            def group(k):
+            def gain_and_bias(k):
                 normed_t = normed_t_of.pop(k)
                 for h in range(2):
                     nc.scalar.activation(
                         out=planes[:, tiles_of(k), 2 + h, :], in_=normed_t[:, h, :, :], func=ACT.Identity,
                         bias=gain_bias[:, 2 + h : 3 + h], scale=gain_bias[:, h : h + 1],
                     )
+
+            def group(k):
                 grouped = work.tile([P, PAIR, P, PACK], BF16, align_bytes=64)
-                nc.scalar.copy(out=grouped[:], in_=planes[:, tiles_of(k), :, :].rearrange("q a t m -> q a m t"))
+                nc.gpsimd.tensor_scalar(
+                    out=grouped[:], in0=planes[:, tiles_of(k), :, :].rearrange("q a t m -> q a m t"),
+                    scalar1=1.0, scalar2=0.0, op0=ALU.mult, op1=ALU.add,
+                )
                 grouped_of[k] = grouped
 
             def quantise(k):
@@ -228,6 +233,9 @@ def tile_edgeupdaterwrapper_v01_pa_t_kernel(tc, p, x_down, ln_edge_g, ln_edge_b,
                     prepare_weights()
                 if is_pair(n - LAG):
                     quantise(n - LAG)
+                if is_pair(n - 1):
+                    gain_and_bias(n - 1)
+                    group(n - 1)
                 if is_pair(n + 1):
                     scale(n + 1)
                 if is_pair(n):
@@ -246,8 +254,6 @@ def tile_edgeupdaterwrapper_v01_pa_t_kernel(tc, p, x_down, ln_edge_g, ln_edge_b,
                     sums(n + 2)
                 if is_pair(n + 1):
                     shift_by_mean(n + 1)
-                if is_pair(n - 1):
-                    group(n - 1)
                 if is_tile(first):
                     add_bias(first, 0)
                 if is_pair(n + 2):

@@ -73,18 +73,20 @@ def tile_edgeupdaterwrapper_v01_pa_t_kernel(tc, p, x_down, ln_edge_g, ln_edge_b,
 
         planes = keep.tile([P, TILES, PACK, P], BF16)
         x_j_view = x_t[:].rearrange("q (a t) -> q t a", t=TILES)
-        for c in range(TILES // FILL):
+
+        def fill_node_plane(c, side):
             ts = slice(c * FILL, (c + 1) * FILL)
+            if side == 0:
+                source = x_t[:].unsqueeze(1).unsqueeze(3).to_broadcast([P, FILL, NODES, 2])
+            else:
+                source = x_j_view[:, ts, :].unsqueeze(2).to_broadcast([P, FILL, NODES, 2])
             nc.gpsimd.tensor_scalar(
-                out=planes[:, ts, 0, :].rearrange("q t (i a) -> q t i a", a=2),
-                in0=x_t[:].unsqueeze(1).unsqueeze(3).to_broadcast([P, FILL, NODES, 2]),
+                out=planes[:, ts, side, :].rearrange("q t (i a) -> q t i a", a=2), in0=source,
                 scalar1=1.0, scalar2=0.0, op0=ALU.mult, op1=ALU.add,
             )
-            nc.gpsimd.tensor_scalar(
-                out=planes[:, ts, 1, :].rearrange("q t (i a) -> q t i a", a=2),
-                in0=x_j_view[:, ts, :].unsqueeze(2).to_broadcast([P, FILL, NODES, 2]),
-                scalar1=1.0, scalar2=0.0, op0=ALU.mult, op1=ALU.add,
-            )
+
+        fill_node_plane(0, 0)
+        fill_node_plane(0, 1)
 
         w_grouped = keep.tile([P, F, PACK], BF16, align_bytes=64)
         w_codes = keep.tile([P, F], U32, align_bytes=64)
@@ -250,6 +252,8 @@ def tile_edgeupdaterwrapper_v01_pa_t_kernel(tc, p, x_down, ln_edge_g, ln_edge_b,
                     add_bias(first - 1, 1)
                 if is_tile(first - 2):
                     relu_and_store(first - 2)
+                if n % 2 == 0 and n // 2 + 2 < 2 * (TILES // FILL):
+                    fill_node_plane((n // 2 + 2) // 2, (n // 2 + 2) % 2)
                 if is_pair(n + 2):
                     sums(n + 2)
                 if is_pair(n + 1):

import concourse.mybir as mybir
from concourse.masks import make_identity

F32 = mybir.dt.float32
BF16 = mybir.dt.bfloat16
U32 = mybir.dt.uint32
U8 = mybir.dt.uint8
FP8X4 = mybir.dt.float8_e4m3fn_x4
ALU = mybir.AluOpType
ACT = mybir.ActivationFunctionType

P = 128
PACK = 4
NODES = 64
HD = 128
ED = 256
F = 1024
EDGES = NODES * NODES
TILES = EDGES // P
N_BANK = 512
EPS = 1e-5
PAIR = 2
PAIRS = TILES // PAIR
LOAD = 4
FILL = 8
LAG = 2
SCALAR_COLS = 768

FLOPS = 2 * EDGES * (2 * HD + ED) * F


def tile_edgeupdaterwrapper_v01_pa_t_kernel(tc, p, x_down, ln_edge_g, ln_edge_b, W1, b1, out):
    nc = tc.nc
    p_view = p.rearrange("b i j f -> (b i j) f").rearrange("(m t) f -> m t f", t=TILES)
    out_view = out.rearrange("b i j f -> (b i j) f").rearrange("(m t) f -> m t f", t=TILES)

    with tc.manual_schedule(), tc.tile_pool(name="keep", bufs=1) as keep:
        small = keep.tile([P, HD], BF16)
        nc.vector.memset(small[NODES:P, :], 0.0)
        nc.sync.dma_start(out=small[0:NODES, :], in_=x_down.rearrange("b n f -> (b n) f"))
        nc.sync.dma_start(out=small[NODES : NODES + 2, :], in_=ln_edge_g.rearrange("(h q) -> h q", q=P))
        nc.sync.dma_start(out=small[NODES + 2 : NODES + 4, :], in_=ln_edge_b.rearrange("(h q) -> h q", q=P))
        w_view = W1.rearrange("(t q) n -> q t n", q=P)
        w_raw = keep.tile([P, PACK, F], BF16)
        p_sb = keep.tile([P, TILES, ED], BF16)
        b1_bc = keep.tile([P, F], BF16)

        def load_p(c):
            nc.sync.dma_start(out=p_sb[:, c * LOAD : (c + 1) * LOAD, :], in_=p_view[:, c * LOAD : (c + 1) * LOAD, :])

        load_p(0)
        load_p(1)
        nc.sync.dma_start(out=w_raw[:, :, 0:N_BANK], in_=w_view[:, :, 0:N_BANK])
        nc.sync.dma_start(out=w_raw[:, :, N_BANK:F], in_=w_view[:, :, N_BANK:F])
        nc.sync.dma_start(out=b1_bc[:], in_=b1.partition_broadcast(P))
        for c in range(2, TILES // LOAD):
            load_p(c)

        ident_bf = keep.tile([P, P], BF16)
        make_identity(nc, ident_bf[:])
        ident_f32 = keep.tile([P, P], F32)
        make_identity(nc, ident_f32[:])
        eps = keep.tile([P, 1], F32)
        nc.vector.memset(eps[:], EPS)

        x_t = keep.tile([P, NODES], BF16)
        gain_bias = keep.tile([P, 4], F32)
        with tc.psum_pool(name="psum_setup", bufs=1) as psum_setup:
            small_t = psum_setup.tile([P, P], BF16)
            nc.tensor.transpose(out=small_t[:], in_=small[:], identity=ident_bf[:])
            nc.vector.tensor_copy(out=x_t[:], in_=small_t[:, 0:NODES])
            nc.vector.tensor_copy(out=gain_bias[:], in_=small_t[:, NODES : NODES + 4])

        planes = keep.tile([P, TILES, PACK, P], BF16)
        x_j_view = x_t[:].rearrange("q (a t) -> q t a", t=TILES)

        def fill_node_plane(c, side):
            ts = slice(c * FILL, (c + 1) * FILL)
            if side == 0:
                source = x_t[:].unsqueeze(1).unsqueeze(3).to_broadcast([P, FILL, NODES, 2])
            else:
                source = x_j_view[:, ts, :].unsqueeze(2).to_broadcast([P, FILL, NODES, 2])
            nc.gpsimd.tensor_scalar(
                out=planes[:, ts, side, :].rearrange("q t (i a) -> q t i a", a=2), in0=source,
                scalar1=1.0, scalar2=0.0, op0=ALU.mult, op1=ALU.add,
            )

        fill_node_plane(0, 0)
        fill_node_plane(0, 1)

        w_grouped = keep.tile([P, F, PACK], BF16, align_bytes=64)
        w_codes = keep.tile([P, F], U32, align_bytes=64)
        w_scales = keep.tile([P, F], U8, align_bytes=64)

        def prepare_weights():
            for nh in range(F // N_BANK):
                cols = slice(nh * N_BANK, (nh + 1) * N_BANK)
                nc.vector.tensor_copy(out=w_grouped[:, cols, :], in_=w_raw[:, :, cols].rearrange("q t n -> q n t"))
            for nh in range(F // N_BANK):
                cols = slice(nh * N_BANK, (nh + 1) * N_BANK)
                nc.vector.quantize_mx(
                    out=w_codes[:, cols].bitcast(FP8X4),
                    scales=w_scales[:, cols],
                    in_=w_grouped[:, cols, :].rearrange("q n t -> q (n t)"),
                )

        stats = keep.tile([P, TILES, 6], F32)
        mean_var = keep.tile([P, TILES, 2], F32)
        rstd = keep.tile([P, TILES], F32)
        shift = keep.tile([P, TILES], F32)

        with tc.tile_pool(name="work", bufs=3) as work, tc.tile_pool(name="outs", bufs=8) as outs, \
                tc.psum_pool(name="psum_t", bufs=2) as psum_t, tc.psum_pool(name="psum_mm", bufs=6) as psum_mm:
            normed_of = {}
            normed_t_of = {}
            grouped_of = {}
            z_of = {}
            acc_of = {}
            result_of = {}

            def tiles_of(k):
                return slice(k * PAIR, (k + 1) * PAIR)

            def sums(k):
                for t in range(k * PAIR, (k + 1) * PAIR):
                    nc.vector.bn_stats(out=stats[:, t, :], in_=p_sb[:, t, :])

            def mean_and_variance(k):
                for t in range(k * PAIR, (k + 1) * PAIR):
                    nc.vector.bn_aggr(out=mean_var[:, t, :], in_=stats[:, t, :])

            def scale(k):
                ts = tiles_of(k)
                nc.scalar.activation(
                    out=rstd[:, ts], in_=mean_var[:, ts, 1], func=ACT.Abs_reciprocal_sqrt, bias=eps[:, 0:1], scale=1.0
                )

            def shift_by_mean(k):
                ts = tiles_of(k)
                nc.vector.scalar_tensor_tensor(
                    out=shift[:, ts], in0=mean_var[:, ts, 0], scalar=-1.0, in1=rstd[:, ts], op0=ALU.mult, op1=ALU.mult
                )

            def normalise(k):
                normed = work.tile([P, PAIR, ED], F32)
                for a in range(PAIR):
                    t = k * PAIR + a
                    nc.scalar.activation(
                        out=normed[:, a, :], in_=p_sb[:, t, :], func=ACT.Identity,
                        bias=shift[:, t : t + 1], scale=rstd[:, t : t + 1],
                    )
                normed_of[k] = normed

            def transpose(k):
                normed = normed_of.pop(k)
                normed_t = psum_t.tile([P, 2, PAIR, P], F32)
                for h in range(2):
                    for a in range(PAIR):
                        nc.tensor.transpose(
                            out=normed_t[:, h, a, :], in_=normed[:, a, h * P : (h + 1) * P], identity=ident_f32[:]
                        )
                normed_t_of[k] = normed_t

            def gain_and_bias(k):
                normed_t = normed_t_of.pop(k)
                for h in range(2):
                    nc.scalar.activation(
                        out=planes[:, tiles_of(k), 2 + h, :], in_=normed_t[:, h, :, :], func=ACT.Identity,
                        bias=gain_bias[:, 2 + h : 3 + h], scale=gain_bias[:, h : h + 1],
                    )

            def group(k):
                grouped = work.tile([P, PAIR, P, PACK], BF16, align_bytes=64)
                nc.gpsimd.tensor_scalar(
                    out=grouped[:], in0=planes[:, tiles_of(k), :, :].rearrange("q a t m -> q a m t"),
                    scalar1=1.0, scalar2=0.0, op0=ALU.mult, op1=ALU.add,
                )
                grouped_of[k] = grouped

            def quantise(k):
                grouped = grouped_of.pop(k)
                z_codes = work.tile([P, PAIR * P], U32, align_bytes=64)
                z_scales = work.tile([P, PAIR * P], U8, align_bytes=64)
                nc.vector.quantize_mx(
                    out=z_codes[:].bitcast(FP8X4), scales=z_scales[:], in_=grouped[:].rearrange("q a m t -> q (a m t)")
                )
                z_of[k] = (z_codes, z_scales)

            def multiply(t):
                z_codes, z_scales = z_of[t // PAIR]
                edges = slice((t % PAIR) * P, (t % PAIR + 1) * P)
                for nh in range(F // N_BANK):
                    cols = slice(nh * N_BANK, (nh + 1) * N_BANK)
                    acc = psum_mm.tile([P, N_BANK], F32)
                    nc.tensor.matmul_mx(
                        out=acc[:],
                        lhsT=z_codes[:, edges].bitcast(FP8X4), lhsT_scale=z_scales[:, edges],
                        rhs=w_codes[:, cols].bitcast(FP8X4), rhs_scale=w_scales[:, cols],
                        start=True, stop=True,
                    )
                    acc_of[(t, nh)] = acc

            def add_bias(t, nh):
                if nh == 0:
                    result_of[t] = outs.tile([P, F], F32, name="result")
                cols = slice(nh * N_BANK, (nh + 1) * N_BANK)
                nc.vector.tensor_tensor(
                    out=result_of[t][:, cols], in0=acc_of.pop((t, nh))[:], in1=b1_bc[:, cols], op=ALU.add
                )

            def relu_and_store(t):
                result = result_of.pop(t)
                nc.scalar.activation(out=result[:, 0:SCALAR_COLS], in_=result[:, 0:SCALAR_COLS], func=ACT.Relu)
                nc.gpsimd.tensor_scalar(
                    out=result[:, SCALAR_COLS:F], in0=result[:, SCALAR_COLS:F],
                    scalar1=float("inf"), scalar2=0.0, op0=ALU.min, op1=ALU.max,
                )
                nc.sync.dma_start(out=out_view[:, t, :], in_=result[:])

            def is_pair(k):
                return 0 <= k < PAIRS

            def is_tile(t):
                return 0 <= t < TILES

            for k in range(2):
                sums(k)
            for k in range(2):
                mean_and_variance(k)
            scale(0)
            shift_by_mean(0)
            for n in range(PAIRS + 3):
                first = (n - LAG) * PAIR
                if n == LAG:
                    prepare_weights()
                if is_pair(n - LAG):
                    quantise(n - LAG)
                if is_pair(n - 1):
                    gain_and_bias(n - 1)
                    group(n - 1)
                if is_pair(n + 1):
                    scale(n + 1)
                if is_pair(n):
                    normalise(n)
                if is_pair(n - LAG):
                    multiply(first)
                    multiply(first + 1)
                if is_pair(n):
                    transpose(n)
                if is_tile(first - 1):
                    add_bias(first - 1, 0)
                    add_bias(first - 1, 1)
                if is_tile(first - 2):
                    relu_and_store(first - 2)
                if n % 2 == 0 and n // 2 + 2 < 2 * (TILES // FILL):
                    fill_node_plane((n // 2 + 2) // 2, (n // 2 + 2) % 2)
                if is_pair(n + 2):
                    sums(n + 2)
                if is_pair(n + 1):
                    shift_by_mean(n + 1)
                if is_tile(first):
                    add_bias(first, 0)
                if is_pair(n + 2):
                    mean_and_variance(n + 2)
                if is_tile(first):
                    add_bias(first, 1)
                if is_tile(first - 1):
                    relu_and_store(first - 1)
